import numpy as np
import ml_dtypes


def mxq(x, axis, fmt="e4m3"):
    dtype, down = {"e4m3": (ml_dtypes.float8_e4m3fn, 7), "e5m2": (ml_dtypes.float8_e5m2, 14)}[fmt]
    v = np.moveaxis(np.asarray(x, np.float32).astype(ml_dtypes.bfloat16).astype(np.float64), axis, -1)
    blocks = v.reshape(v.shape[:-1] + (-1, 32))
    amax = np.abs(blocks).max(-1, keepdims=True)
    byte = np.maximum(np.where(amax > 0, np.frexp(amax)[1] - 1 + 127, 0) - down, 1)
    scale = np.exp2(byte - 127.0)
    codes = (blocks / scale).astype(np.float32).astype(dtype).astype(np.float64)
    return np.moveaxis((codes * scale).reshape(v.shape), -1, axis)


WIDE = False


def mx_kscale(k):
    if not WIDE:
        return np.ones(k)
    levels = np.array([10, -10, 5, -5, 0])
    a = np.random.permutation(np.resize(levels, k // 512 * 4)).reshape(k // 512, 4)
    idx = np.arange(k)
    return np.exp2(a[idx // 512, idx % 128 // 32])


BF16 = ml_dtypes.bfloat16


def bf(x):
    return np.asarray(x, np.float32).astype(BF16)


def f64(x):
    return np.asarray(x).astype(np.float64)


P, D, B = 8, 512, 128
LAMBDA = 0.1
JJ, II = np.nonzero(1 - np.eye(P, dtype=np.int64))


def setup_inputs():
    s = mx_kscale(D)
    s = s / s.max()
    return {"F": bf(np.random.standard_normal((P, D, B)) * s[:, None]),
            "R": bf(np.random.standard_normal((P, P, D, D)) / np.sqrt(D * (P - 1)) / s)}


def reference(F, R):
    p = F.shape[0]
    Fq = mxq(f64(F), 1, "e4m3")
    Rq = mxq(f64(R)[II, JJ], 2, "e4m3")
    Fi = Fq[II]
    agg = Rq.reshape(P, P - 1, D, D).transpose(0, 2, 1, 3).reshape(P, D, (P - 1) * D) @ Fi.reshape(P, (P - 1) * D, B)
    updated = (f64(F) + agg) / p
    M = np.zeros((P, P, D, B))
    M[II, JJ] = Rq @ Fi
    Dif = M - M.swapaxes(0, 1)
    loss = LAMBDA * 0.5 * np.sum(Dif * Dif)
    return updated, loss

@@ -1,0 +1,222 @@
+from contextlib import ExitStack
+
+import concourse.mybir as mybir
+from concourse.masks import make_identity
+
+F32 = mybir.dt.float32
+BF16 = mybir.dt.bfloat16
+U32 = mybir.dt.uint32
+U8 = mybir.dt.uint8
+FP8X4 = mybir.dt.float8_e4m3fn_x4
+ALU = mybir.AluOpType
+ACT = mybir.ActivationFunctionType
+
+NP = 8
+D = 512
+B = 128
+P = 128
+LOSS_WEIGHT = 0.1 * 0.5 * 2.0
+
+FLOPS = 2 * NP * (NP - 1) * D * D * B
+BYTES = NP * (NP - 1) * D * D * 2 + NP * D * B * 2 + NP * D * B * 4 + 4
+
+MANUAL = True
+RAW_BUFS = 4
+GROUPED_BUFS = 2
+
+
+def tile_sheaflayer_kernel(tc, F, R, out_0, out_1):
+    nc = tc.nc
+    units = [(i, j) for i in range(NP) for j in range(i + 1, NP)]
+    n_units = len(units)
+    unit_of = dict((pair, n) for n, pair in enumerate(units))
+    closing = dict((j, unit_of[(min(j, NP - 2), NP - 1)]) for j in range(NP))
+
+    bunch = [[] for n in range(n_units)]
+    for n, (i, j) in enumerate(units):
+        bunch[n].append((i, j))
+    for j in range(1, NP - 1):
+        r = j - 1
+        first = unit_of[(r, r + 1)]
+        n_round = NP - 1 - r
+        for e in range(j):
+            bunch[first + 1 + (e * (n_round - 1)) // j].append((j, e))
+    for e in range(NP - 2):
+        bunch[n_units - 2].append((NP - 1, e))
+    bunch[n_units - 1].append((NP - 1, NP - 2))
+
+    with ExitStack() as ctx:
+        if MANUAL:
+            ctx.enter_context(tc.manual_schedule())
+        keep = ctx.enter_context(tc.tile_pool(name="keep", bufs=1))
+        rawpool = ctx.enter_context(tc.tile_pool(name="rawpool", bufs=RAW_BUFS))
+        gpool = ctx.enter_context(tc.tile_pool(name="gpool", bufs=GROUPED_BUFS))
+        fpool = ctx.enter_context(tc.tile_pool(name="fpool", bufs=2))
+        opool = ctx.enter_context(tc.tile_pool(name="opool", bufs=2))
+        psum = ctx.enter_context(tc.psum_pool(name="psum", bufs=1))
+
+        ident = keep.tile([P, P], F32, name="ident")
+        make_identity(nc, ident[:])
+        zt = keep.tile([P, P], F32, name="zt")
+        nc.vector.memset(zt[:], 0.0)
+        acc = keep.tile([P, n_units], F32, name="acc")
+        tot = keep.tile([P, 1], F32, name="tot")
+        junk = keep.tile([P, D], F32, name="junk")
+        fm = keep.tile([P, NP, D], BF16, name="fm")
+        fcd = [keep.tile([P, B if i == 0 else 2 * B], U32, name="fcd%d" % i, align_bytes=64) for i in range(NP)]
+        fpl = [keep.tile([P, B if i == 0 else 2 * B], U8, name="fpl%d" % i, align_bytes=64) for i in range(NP)]
+        cd = [keep.tile([P, 2 * D], U32, name="cd%d" % n, align_bytes=64) for n in range(n_units)]
+        pl = [keep.tile([P, 2 * D], U8, name="pl%d" % n, align_bytes=64) for n in range(n_units)]
+        raw = {}
+        grouped = {}
+        dif = {}
+        agg = {}
+        agg_done = dict((j, 0) for j in range(NP))
+        aggT = {}
+        fin = {}
+
+        def load_f(i):
+            nc.sync.dma_start(
+                out=fm[:, i, :].rearrange("p (u x) -> p u x", u=2),
+                in_=F[i].rearrange("(u q e) b -> q u (e b)", u=2, e=2),
+            )
+
+        def load_unit(n):
+            i, j = units[n]
+            raw[n] = rawpool.tile([P, 8 * D], BF16, name="raw", tag="raw")
+            nc.sync.dma_start(out=raw[n][:, 0 : 4 * D], in_=R[i, j].rearrange("(p c) e -> p (c e)", c=4))
+            nc.sync.dma_start(out=raw[n][:, 4 * D : 8 * D], in_=R[j, i].rearrange("(p c) e -> p (c e)", c=4))
+
+        def prepare_f(i):
+            width = D if i == 0 else 2 * D
+            fg = fpool.tile([P, width], BF16, name="fg", tag="fg", align_bytes=64)
+            nc.vector.tensor_copy(
+                out=fg[:, 0:D].rearrange("p (b t) -> p b t", t=4),
+                in_=fm[:, i, :].rearrange("p (t b) -> p b t", t=4),
+            )
+            if i > 0:
+                nc.vector.tensor_scalar_mul(out=fg[:, D : 2 * D], in0=fg[:, 0:D], scalar1=-1.0)
+            nc.vector.quantize_mx(out=fcd[i][:].bitcast(FP8X4), scales=fpl[i][:], in_=fg[:])
+
+        def transpose_unit(n):
+            words = raw[n][:].bitcast(F32)
+            grouped[n] = gpool.tile([P, 8 * D], BF16, name="grouped", tag="grouped", align_bytes=64)
+            g32 = grouped[n][:].bitcast(F32)
+            for b in range(4):
+                tb = psum.tile([P, D], F32, name="tb%d" % b, tag="T%d" % b)
+                for x in range(4):
+                    col = D * b + P * x
+                    nc.tensor.transpose(tb[:, P * x : P * (x + 1)], words[:, col : col + P], ident[:])
+                src = tb[:].rearrange("p (c u d) -> p c d u", c=2, u=2)
+                dst = g32[:, D * b : D * (b + 1)].rearrange("p (c d u) -> p c d u", c=2, u=2)
+                if b < 3:
+                    nc.scalar.copy(out=dst, in_=src)
+                else:
+                    nc.vector.tensor_copy(out=dst, in_=src)
+
+        def quantise_unit(n):
+            for s in range(2):
+                nc.vector.quantize_mx(
+                    out=cd[n][:, D * s : D * (s + 1)].bitcast(FP8X4),
+                    scales=pl[n][:, D * s : D * (s + 1)],
+                    in_=grouped[n][:, 4 * D * s : 4 * D * (s + 1)],
+                )
+
+        def mx_pass(bank, i_src, sign, n, s, start, stop):
+            nc.tensor.matmul_mx(
+                out=bank[:],
+                lhsT=fcd[i_src][:, B * sign : B * (sign + 1)].bitcast(FP8X4),
+                lhsT_scale=fpl[i_src][:, B * sign : B * (sign + 1)],
+                rhs=cd[n][:, D * s : D * (s + 1)].bitcast(FP8X4),
+                rhs_scale=pl[n][:, D * s : D * (s + 1)],
+                start=start,
+                stop=stop,
+            )
+
+        def multiply_unit(n):
+            i, j = units[n]
+            dif[n] = psum.tile([P, D], F32, name="dif%d" % (n % 2), tag="D%d" % (n % 2))
+            mx_pass(dif[n], i, 0, n, 0, True, False)
+            mx_pass(dif[n], j, 1, n, 1, False, True)
+            for (dst, i_src) in bunch[n]:
+                if agg_done[dst] == 0:
+                    tag = "T0" if dst == NP - 1 else "A%d" % (dst % 2)
+                    agg[dst] = psum.tile([P, D], F32, name="agg%d" % dst, tag=tag)
+                if i_src < dst:
+                    where, s = unit_of[(i_src, dst)], 0
+                else:
+                    where, s = unit_of[(dst, i_src)], 1
+                mx_pass(agg[dst], i_src, 0, where, s, agg_done[dst] == 0, agg_done[dst] == NP - 2)
+                agg_done[dst] += 1
+
+        def square_unit(n):
+            nc.scalar.activation(out=junk[:], in_=dif[n][:], func=ACT.Square, accum_out=acc[:, n : n + 1])
+
+        def evacuate(j, on_scalar):
+            aggT[j] = opool.tile([P, D], F32, name="aggT", tag="aggT")
+            src = agg[j][:].rearrange("p (r e u a) -> p u e a r", r=2, e=2, u=2)
+            for u in range(2):
+                dst = aggT[j][:, 256 * u : 256 * (u + 1)].rearrange("p (e a r) -> p e a r", e=2, r=2)
+                if on_scalar:
+                    nc.scalar.mul(out=dst, in_=src[:, u], mul=0.125)
+                else:
+                    nc.vector.tensor_scalar_mul(out=dst, in0=src[:, u], scalar1=0.125)
+
+        def transpose_back(j):
+            tag = "T0" if j == NP - 1 else "A%d" % (j % 2)
+            fin[j] = psum.tile([P, D], F32, name="fin%d" % j, tag=tag)
+            for t in range(4):
+                nc.tensor.transpose(fin[j][:, P * t : P * (t + 1)], aggT[j][:, P * t : P * (t + 1)], ident[:])
+
+        def finish(j):
+            res = opool.tile([P, D], F32, name="res", tag="res")
+            nc.vector.scalar_tensor_tensor(
+                out=res[:], in0=fm[:, j, :], scalar=0.125, in1=fin[j][:], op0=ALU.mult, op1=ALU.add
+            )
+            nc.sync.dma_start(
+                out=out_0[j].rearrange("(u q e) b -> q u (e b)", u=2, e=2),
+                in_=res[:].rearrange("p (u x) -> p u x", u=2),
+            )
+
+        load_unit(0)
+        load_f(0)
+        load_f(1)
+        load_f(2)
+        for n in range(1, RAW_BUFS):
+            load_unit(n)
+            if n + 2 < NP:
+                load_f(n + 2)
+
+        for n in range(n_units + 2):
+            closed = [j for j in range(NP) if closing[j] == n - 2]
+            if 0 <= n - 2:
+                square_unit(n - 2)
+            for k, j in enumerate(closed):
+                evacuate(j, k == 1)
+            if n < n_units:
+                transpose_unit(n)
+            for j in closed:
+                transpose_back(j)
+            if n < n_units:
+                quantise_unit(n)
+                if n == 0:
+                    prepare_f(0)
+                if n + 1 < NP:
+                    prepare_f(n + 1)
+            for j in closed:
+                finish(j)
+            if 1 <= n <= n_units:
+                multiply_unit(n - 1)
+            if n + RAW_BUFS < n_units:
+                load_unit(n + RAW_BUFS)
+                if n + RAW_BUFS + 2 < NP:
+                    load_f(n + RAW_BUFS + 2)
+
+        nc.vector.reduce_sum(out=zt[:, 0:1], in_=acc[:], axis=mybir.AxisListType.X)
+        lt = psum.tile([P, D], F32, name="lt", tag="D0")
+        nc.tensor.transpose(lt[:, 0:P], zt[:], ident[:])
+        nc.scalar.activation(out=junk[:, 0:P], in_=lt[:, 0:P], func=ACT.Copy, scale=LOSS_WEIGHT, accum_out=tot[:, 0:1])
+        loss_view = out_1
+        for k in range(2 - len(out_1.shape)):
+            loss_view = loss_view.unsqueeze(0)
+        nc.sync.dma_start(out=loss_view, in_=tot[0:1, 0:1])

@@ -30,20 +30,31 @@ def tile_sheaflayer_kernel(tc, F, R, out_0, out_1):
     units = [(i, j) for i in range(NP) for j in range(i + 1, NP)]
     n_units = len(units)
     unit_of = dict((pair, n) for n, pair in enumerate(units))
-    closing = dict((j, unit_of[(min(j, NP - 2), NP - 1)]) for j in range(NP))
-
-    bunch = [[] for n in range(n_units)]
+    pending = dict((j, []) for j in range(NP))
+    count = dict((j, 0) for j in range(NP))
+    closed_in = {}
+    live = []
+    early = []
     for n, (i, j) in enumerate(units):
-        bunch[n].append((i, j))
-    for j in range(1, NP - 1):
-        r = j - 1
-        first = unit_of[(r, r + 1)]
-        n_round = NP - 1 - r
-        for e in range(j):
-            bunch[first + 1 + (e * (n_round - 1)) // j].append((j, e))
-    for e in range(NP - 2):
-        bunch[n_units - 2].append((NP - 1, e))
-    bunch[n_units - 1].append((NP - 1, NP - 2))
+        pending[j].append(i)
+        pending[i].append(j)
+        live.append([])
+        early.append([])
+        for k in range(NP):
+            if k in closed_in:
+                continue
+            if k == NP - 1:
+                may = n >= n_units - 2
+            else:
+                may = k < 2 or (k - 2 in closed_in and closed_in[k - 2] < n)
+            if not may:
+                continue
+            for i_src in pending[k]:
+                (live if k == i else early)[n].append((k, i_src))
+                count[k] += 1
+            pending[k] = []
+            if count[k] == NP - 1:
+                closed_in[k] = n
 
     with ExitStack() as ctx:
         if MANUAL:
@@ -52,7 +63,7 @@ def tile_sheaflayer_kernel(tc, F, R, out_0, out_1):
         rawpool = ctx.enter_context(tc.tile_pool(name="rawpool", bufs=RAW_BUFS))
         gpool = ctx.enter_context(tc.tile_pool(name="gpool", bufs=GROUPED_BUFS))
         fpool = ctx.enter_context(tc.tile_pool(name="fpool", bufs=2))
-        opool = ctx.enter_context(tc.tile_pool(name="opool", bufs=2))
+        opool = ctx.enter_context(tc.tile_pool(name="opool", bufs=3))
         psum = ctx.enter_context(tc.psum_pool(name="psum", bufs=1))
 
         ident = keep.tile([P, P], F32, name="ident")
@@ -133,12 +144,8 @@ def tile_sheaflayer_kernel(tc, F, R, out_0, out_1):
                 stop=stop,
             )
 
-        def multiply_unit(n):
-            i, j = units[n]
-            dif[n] = psum.tile([P, D], F32, name="dif%d" % (n % 2), tag="D%d" % (n % 2))
-            mx_pass(dif[n], i, 0, n, 0, True, False)
-            mx_pass(dif[n], j, 1, n, 1, False, True)
-            for (dst, i_src) in bunch[n]:
+        def agg_passes(todo):
+            for (dst, i_src) in todo:
                 if agg_done[dst] == 0:
                     tag = "T0" if dst == NP - 1 else "A%d" % (dst % 2)
                     agg[dst] = psum.tile([P, D], F32, name="agg%d" % dst, tag=tag)
@@ -148,6 +155,22 @@ def tile_sheaflayer_kernel(tc, F, R, out_0, out_1):
                     where, s = unit_of[(dst, i_src)], 1
                 mx_pass(agg[dst], i_src, 0, where, s, agg_done[dst] == 0, agg_done[dst] == NP - 2)
                 agg_done[dst] += 1
+
+        def multiply_unit(n):
+            i, j = units[n]
+            closes = [k for k in range(NP) if closed_in[k] == n]
+            if closes:
+                agg_passes(live[n])
+                if n == n_units - 1:
+                    agg_passes(early[n])
+            dif[n] = psum.tile([P, D], F32, name="dif", tag="D")
+            mx_pass(dif[n], i, 0, n, 0, True, False)
+            mx_pass(dif[n], j, 1, n, 1, False, True)
+            if not closes:
+                agg_passes(live[n])
+            if n < n_units - 1:
+                agg_passes(early[n])
+            return closes
 
         def square_unit(n):
             nc.scalar.activation(out=junk[:], in_=dif[n][:], func=ACT.Square, accum_out=acc[:, n : n + 1])
@@ -163,7 +186,7 @@ def tile_sheaflayer_kernel(tc, F, R, out_0, out_1):
                     nc.vector.tensor_scalar_mul(out=dst, in0=src[:, u], scalar1=0.125)
 
         def transpose_back(j):
-            tag = "T0" if j == NP - 1 else "A%d" % (j % 2)
+            tag = "X" if j < NP - 2 else "T%d" % (j - NP + 3)
             fin[j] = psum.tile([P, D], F32, name="fin%d" % j, tag=tag)
             for t in range(4):
                 nc.tensor.transpose(fin[j][:, P * t : P * (t + 1)], aggT[j][:, P * t : P * (t + 1)], ident[:])
@@ -187,33 +210,55 @@ def tile_sheaflayer_kernel(tc, F, R, out_0, out_1):
             if n + 2 < NP:
                 load_f(n + 2)
 
-        for n in range(n_units + 2):
-            closed = [j for j in range(NP) if closing[j] == n - 2]
-            if 0 <= n - 2:
-                square_unit(n - 2)
-            for k, j in enumerate(closed):
-                evacuate(j, k == 1)
-            if n < n_units:
-                transpose_unit(n)
-            for j in closed:
+        waiting = []
+        for n in range(n_units - 1):
+            transpose_unit(n)
+            back = waiting
+            for j in back:
                 transpose_back(j)
-            if n < n_units:
-                quantise_unit(n)
-                if n == 0:
-                    prepare_f(0)
-                if n + 1 < NP:
-                    prepare_f(n + 1)
-            for j in closed:
+            waiting = []
+            if n >= 2:
+                waiting = multiply_unit(n - 2)
+                square_unit(n - 2)
+                for j in waiting:
+                    evacuate(j, False)
+            quantise_unit(n)
+            if n == 0:
+                prepare_f(0)
+            if n + 1 < NP:
+                prepare_f(n + 1)
+            for j in back:
                 finish(j)
-            if 1 <= n <= n_units:
-                multiply_unit(n - 1)
             if n + RAW_BUFS < n_units:
                 load_unit(n + RAW_BUFS)
                 if n + RAW_BUFS + 2 < NP:
                     load_f(n + RAW_BUFS + 2)
 
+        n = n_units - 1
+        transpose_unit(n)
+        for j in waiting:
+            transpose_back(j)
+        quantise_unit(n)
+        for j in waiting:
+            finish(j)
+        multiply_unit(n - 2)
+        square_unit(n - 2)
+        multiply_unit(n - 1)
+        square_unit(n - 1)
+        evacuate(NP - 3, False)
+        transpose_back(NP - 3)
+        finish(NP - 3)
+        multiply_unit(n)
+        evacuate(NP - 2, False)
+        evacuate(NP - 1, True)
+        square_unit(n)
+        transpose_back(NP - 2)
+        transpose_back(NP - 1)
+        finish(NP - 2)
         nc.vector.reduce_sum(out=zt[:, 0:1], in_=acc[:], axis=mybir.AxisListType.X)
-        lt = psum.tile([P, D], F32, name="lt", tag="D0")
+        finish(NP - 1)
+
+        lt = psum.tile([P, D], F32, name="lt", tag="T3")
         nc.tensor.transpose(lt[:, 0:P], zt[:], ident[:])
         nc.scalar.activation(out=junk[:, 0:P], in_=lt[:, 0:P], func=ACT.Copy, scale=LOSS_WEIGHT, accum_out=tot[:, 0:1])
         loss_view = out_1

@@ -79,6 +79,7 @@ def tile_sheaflayer_kernel(tc, F, R, out_0, out_1):
         cd = [keep.tile([P, 2 * D], U32, name="cd%d" % n, align_bytes=64) for n in range(n_units)]
         pl = [keep.tile([P, 2 * D], U8, name="pl%d" % n, align_bytes=64) for n in range(n_units)]
         raw = {}
+        fg = {}
         grouped = {}
         dif = {}
         agg = {}
@@ -98,16 +99,20 @@ def tile_sheaflayer_kernel(tc, F, R, out_0, out_1):
             nc.sync.dma_start(out=raw[n][:, 0 : 4 * D], in_=R[i, j].rearrange("(p c) e -> p (c e)", c=4))
             nc.sync.dma_start(out=raw[n][:, 4 * D : 8 * D], in_=R[j, i].rearrange("(p c) e -> p (c e)", c=4))
 
-        def prepare_f(i):
+        def regroup_f(i):
             width = D if i == 0 else 2 * D
-            fg = fpool.tile([P, width], BF16, name="fg", tag="fg", align_bytes=64)
+            fg[i] = fpool.tile([P, width], BF16, name="fg", tag="fg", align_bytes=64)
             nc.vector.tensor_copy(
-                out=fg[:, 0:D].rearrange("p (b t) -> p b t", t=4),
+                out=fg[i][:, 0:D].rearrange("p (b t) -> p b t", t=4),
                 in_=fm[:, i, :].rearrange("p (t b) -> p b t", t=4),
             )
+
+        def negate_f(i):
             if i > 0:
-                nc.vector.tensor_scalar_mul(out=fg[:, D : 2 * D], in0=fg[:, 0:D], scalar1=-1.0)
-            nc.vector.quantize_mx(out=fcd[i][:].bitcast(FP8X4), scales=fpl[i][:], in_=fg[:])
+                nc.vector.tensor_scalar_mul(out=fg[i][:, D : 2 * D], in0=fg[i][:, 0:D], scalar1=-1.0)
+
+        def quantise_f(i):
+            nc.vector.quantize_mx(out=fcd[i][:].bitcast(FP8X4), scales=fpl[i][:], in_=fg[i][:])
 
         def transpose_unit(n):
             words = raw[n][:].bitcast(F32)
@@ -125,13 +130,12 @@ def tile_sheaflayer_kernel(tc, F, R, out_0, out_1):
                 else:
                     nc.vector.tensor_copy(out=dst, in_=src)
 
-        def quantise_unit(n):
-            for s in range(2):
-                nc.vector.quantize_mx(
-                    out=cd[n][:, D * s : D * (s + 1)].bitcast(FP8X4),
-                    scales=pl[n][:, D * s : D * (s + 1)],
-                    in_=grouped[n][:, 4 * D * s : 4 * D * (s + 1)],
-                )
+        def quantise_block(n, s):
+            nc.vector.quantize_mx(
+                out=cd[n][:, D * s : D * (s + 1)].bitcast(FP8X4),
+                scales=pl[n][:, D * s : D * (s + 1)],
+                in_=grouped[n][:, 4 * D * s : 4 * D * (s + 1)],
+            )
 
         def mx_pass(bank, i_src, sign, n, s, start, stop):
             nc.tensor.matmul_mx(
@@ -222,11 +226,15 @@ def tile_sheaflayer_kernel(tc, F, R, out_0, out_1):
                 square_unit(n - 2)
                 for j in waiting:
                     evacuate(j, False)
-            quantise_unit(n)
-            if n == 0:
-                prepare_f(0)
-            if n + 1 < NP:
-                prepare_f(n + 1)
+            new_f = [i for i in range(NP) if (i == 0 and n == 0) or i == n + 1]
+            for i in new_f:
+                regroup_f(i)
+            quantise_block(n, 0)
+            for i in new_f:
+                negate_f(i)
+            quantise_block(n, 1)
+            for i in new_f:
+                quantise_f(i)
             for j in back:
                 finish(j)
             if n + RAW_BUFS < n_units:
@@ -238,7 +246,8 @@ def tile_sheaflayer_kernel(tc, F, R, out_0, out_1):
         transpose_unit(n)
         for j in waiting:
             transpose_back(j)
-        quantise_unit(n)
+        quantise_block(n, 0)
+        quantise_block(n, 1)
         for j in waiting:
             finish(j)
         multiply_unit(n - 2)

@@ -23,6 +23,7 @@ BYTES = NP * (NP - 1) * D * D * 2 + NP * D * B * 2 + NP * D * B * 4 + 4
 MANUAL = True
 RAW_BUFS = 4
 GROUPED_BUFS = 2
+SCALAR_TAKES_ALL = (0, 1, 3, 5)
 
 
 def tile_sheaflayer_kernel(tc, F, R, out_0, out_1):
@@ -125,7 +126,7 @@ def tile_sheaflayer_kernel(tc, F, R, out_0, out_1):
                     nc.tensor.transpose(tb[:, P * x : P * (x + 1)], words[:, col : col + P], ident[:])
                 src = tb[:].rearrange("p (c u d) -> p c d u", c=2, u=2)
                 dst = g32[:, D * b : D * (b + 1)].rearrange("p (c d u) -> p c d u", c=2, u=2)
-                if b < 3:
+                if b < 3 or n in SCALAR_TAKES_ALL:
                     nc.scalar.copy(out=dst, in_=src)
                 else:
                     nc.vector.tensor_copy(out=dst, in_=src)

@@ -23,6 +23,8 @@ BYTES = NP * (NP - 1) * D * D * 2 + NP * D * B * 2 + NP * D * B * 4 + 4
 MANUAL = True
 RAW_BUFS = 4
 GROUPED_BUFS = 2
+PAD = 48
+SLOT = 256
 SCALAR_TAKES_ALL = (0, 1, 3, 5)
 
 
@@ -67,18 +69,18 @@ def tile_sheaflayer_kernel(tc, F, R, out_0, out_1):
         opool = ctx.enter_context(tc.tile_pool(name="opool", bufs=3))
         psum = ctx.enter_context(tc.psum_pool(name="psum", bufs=1))
 
+        cd = [keep.tile([P, 2 * D], U32, name="cd%d" % n, align_bytes=256 if n == 0 else 64) for n in range(n_units)]
+        pl = [keep.tile([P, 2 * D], U8, name="pl%d" % n, align_bytes=64) for n in range(n_units)]
+        fcd = [keep.tile([P, 320], U32, name="fcd%d" % i, align_bytes=64) for i in range(NP)]
+        fpl = [keep.tile([P, 2 * SLOT], U8, name="fpl%d" % i, align_bytes=64) for i in range(NP)]
         ident = keep.tile([P, P], F32, name="ident")
         make_identity(nc, ident[:])
         zt = keep.tile([P, P], F32, name="zt")
         nc.vector.memset(zt[:], 0.0)
+        fm = keep.tile([P, NP, D], BF16, name="fm")
+        junk = keep.tile([P, D], F32, name="junk")
         acc = keep.tile([P, n_units], F32, name="acc")
         tot = keep.tile([P, 1], F32, name="tot")
-        junk = keep.tile([P, D], F32, name="junk")
-        fm = keep.tile([P, NP, D], BF16, name="fm")
-        fcd = [keep.tile([P, B if i == 0 else 2 * B], U32, name="fcd%d" % i, align_bytes=64) for i in range(NP)]
-        fpl = [keep.tile([P, B if i == 0 else 2 * B], U8, name="fpl%d" % i, align_bytes=64) for i in range(NP)]
-        cd = [keep.tile([P, 2 * D], U32, name="cd%d" % n, align_bytes=64) for n in range(n_units)]
-        pl = [keep.tile([P, 2 * D], U8, name="pl%d" % n, align_bytes=64) for n in range(n_units)]
         raw = {}
         fg = {}
         grouped = {}
@@ -112,8 +114,13 @@ def tile_sheaflayer_kernel(tc, F, R, out_0, out_1):
             if i > 0:
                 nc.vector.tensor_scalar_mul(out=fg[i][:, D : 2 * D], in0=fg[i][:, 0:D], scalar1=-1.0)
 
-        def quantise_f(i):
-            nc.vector.quantize_mx(out=fcd[i][:].bitcast(FP8X4), scales=fpl[i][:], in_=fg[i][:])
+        def quantise_f(i, sign):
+            if i > 0 or sign == 0:
+                nc.vector.quantize_mx(
+                    out=fcd[i][:, PAD + B * sign : PAD + B * (sign + 1)].bitcast(FP8X4),
+                    scales=fpl[i][:, SLOT * sign : SLOT * sign + B],
+                    in_=fg[i][:, D * sign : D * (sign + 1)],
+                )
 
         def transpose_unit(n):
             words = raw[n][:].bitcast(F32)
@@ -141,8 +148,8 @@ def tile_sheaflayer_kernel(tc, F, R, out_0, out_1):
         def mx_pass(bank, i_src, sign, n, s, start, stop):
             nc.tensor.matmul_mx(
                 out=bank[:],
-                lhsT=fcd[i_src][:, B * sign : B * (sign + 1)].bitcast(FP8X4),
-                lhsT_scale=fpl[i_src][:, B * sign : B * (sign + 1)],
+                lhsT=fcd[i_src][:, PAD + B * sign : PAD + B * (sign + 1)].bitcast(FP8X4),
+                lhsT_scale=fpl[i_src][:, SLOT * sign : SLOT * sign + B],
                 rhs=cd[n][:, D * s : D * (s + 1)].bitcast(FP8X4),
                 rhs_scale=pl[n][:, D * s : D * (s + 1)],
                 start=start,
@@ -233,9 +240,11 @@ def tile_sheaflayer_kernel(tc, F, R, out_0, out_1):
             quantise_block(n, 0)
             for i in new_f:
                 negate_f(i)
+            for i in new_f:
+                quantise_f(i, 0)
             quantise_block(n, 1)
             for i in new_f:
-                quantise_f(i)
+                quantise_f(i, 1)
             for j in back:
                 finish(j)
             if n + RAW_BUFS < n_units:

from contextlib import ExitStack

import concourse.mybir as mybir
from concourse.masks import make_identity

F32 = mybir.dt.float32
BF16 = mybir.dt.bfloat16
U32 = mybir.dt.uint32
U8 = mybir.dt.uint8
FP8X4 = mybir.dt.float8_e4m3fn_x4
ALU = mybir.AluOpType
ACT = mybir.ActivationFunctionType

NP = 8
D = 512
B = 128
P = 128
LOSS_WEIGHT = 0.1 * 0.5 * 2.0

FLOPS = 2 * NP * (NP - 1) * D * D * B
BYTES = NP * (NP - 1) * D * D * 2 + NP * D * B * 2 + NP * D * B * 4 + 4

MANUAL = True
RAW_BUFS = 4
GROUPED_BUFS = 2
PAD = 48
SLOT = 256
SCALAR_TAKES_ALL = (0, 1, 3, 5)


def tile_sheaflayer_kernel(tc, F, R, out_0, out_1):
    nc = tc.nc
    units = [(i, j) for i in range(NP) for j in range(i + 1, NP)]
    n_units = len(units)
    unit_of = dict((pair, n) for n, pair in enumerate(units))
    pending = dict((j, []) for j in range(NP))
    count = dict((j, 0) for j in range(NP))
    closed_in = {}
    live = []
    early = []
    for n, (i, j) in enumerate(units):
        pending[j].append(i)
        pending[i].append(j)
        live.append([])
        early.append([])
        for k in range(NP):
            if k in closed_in:
                continue
            if k == NP - 1:
                may = n >= n_units - 2
            else:
                may = k < 2 or (k - 2 in closed_in and closed_in[k - 2] < n)
            if not may:
                continue
            for i_src in pending[k]:
                (live if k == i else early)[n].append((k, i_src))
                count[k] += 1
            pending[k] = []
            if count[k] == NP - 1:
                closed_in[k] = n

    with ExitStack() as ctx:
        if MANUAL:
            ctx.enter_context(tc.manual_schedule())
        keep = ctx.enter_context(tc.tile_pool(name="keep", bufs=1))
        rawpool = ctx.enter_context(tc.tile_pool(name="rawpool", bufs=RAW_BUFS))
        gpool = ctx.enter_context(tc.tile_pool(name="gpool", bufs=GROUPED_BUFS))
        fpool = ctx.enter_context(tc.tile_pool(name="fpool", bufs=2))
        opool = ctx.enter_context(tc.tile_pool(name="opool", bufs=3))
        psum = ctx.enter_context(tc.psum_pool(name="psum", bufs=1))

        cd = [keep.tile([P, 2 * D], U32, name="cd%d" % n, align_bytes=256 if n == 0 else 64) for n in range(n_units)]
        pl = [keep.tile([P, 2 * D], U8, name="pl%d" % n, align_bytes=64) for n in range(n_units)]
        fcd = [keep.tile([P, 320], U32, name="fcd%d" % i, align_bytes=64) for i in range(NP)]
        fpl = [keep.tile([P, 2 * SLOT], U8, name="fpl%d" % i, align_bytes=64) for i in range(NP)]
        ident = keep.tile([P, P], F32, name="ident")
        make_identity(nc, ident[:])
        zt = keep.tile([P, P], F32, name="zt")
        nc.vector.memset(zt[:], 0.0)
        fm = keep.tile([P, NP, D], BF16, name="fm")
        junk = keep.tile([P, D], F32, name="junk")
        acc = keep.tile([P, n_units], F32, name="acc")
        tot = keep.tile([P, 1], F32, name="tot")
        raw = {}
        fg = {}
        grouped = {}
        dif = {}
        agg = {}
        agg_done = dict((j, 0) for j in range(NP))
        aggT = {}
        fin = {}

        def load_f(i):
            nc.sync.dma_start(
                out=fm[:, i, :].rearrange("p (u x) -> p u x", u=2),
                in_=F[i].rearrange("(u q e) b -> q u (e b)", u=2, e=2),
            )

        def load_unit(n):
            i, j = units[n]
            raw[n] = rawpool.tile([P, 8 * D], BF16, name="raw", tag="raw")
            nc.sync.dma_start(out=raw[n][:, 0 : 4 * D], in_=R[i, j].rearrange("(p c) e -> p (c e)", c=4))
            nc.sync.dma_start(out=raw[n][:, 4 * D : 8 * D], in_=R[j, i].rearrange("(p c) e -> p (c e)", c=4))

        def regroup_f(i):
            width = D if i == 0 else 2 * D
            fg[i] = fpool.tile([P, width], BF16, name="fg", tag="fg", align_bytes=64)
            nc.vector.tensor_copy(
                out=fg[i][:, 0:D].rearrange("p (b t) -> p b t", t=4),
                in_=fm[:, i, :].rearrange("p (t b) -> p b t", t=4),
            )

        def negate_f(i):
            if i > 0:
                nc.vector.tensor_scalar_mul(out=fg[i][:, D : 2 * D], in0=fg[i][:, 0:D], scalar1=-1.0)

        def quantise_f(i, sign):
            if i > 0 or sign == 0:
                nc.vector.quantize_mx(
                    out=fcd[i][:, PAD + B * sign : PAD + B * (sign + 1)].bitcast(FP8X4),
                    scales=fpl[i][:, SLOT * sign : SLOT * sign + B],
                    in_=fg[i][:, D * sign : D * (sign + 1)],
                )

        def transpose_unit(n):
            words = raw[n][:].bitcast(F32)
            grouped[n] = gpool.tile([P, 8 * D], BF16, name="grouped", tag="grouped", align_bytes=64)
            g32 = grouped[n][:].bitcast(F32)
            for b in range(4):
                tb = psum.tile([P, D], F32, name="tb%d" % b, tag="T%d" % b)
                for x in range(4):
                    col = D * b + P * x
                    nc.tensor.transpose(tb[:, P * x : P * (x + 1)], words[:, col : col + P], ident[:])
                src = tb[:].rearrange("p (c u d) -> p c d u", c=2, u=2)
                dst = g32[:, D * b : D * (b + 1)].rearrange("p (c d u) -> p c d u", c=2, u=2)
                if b < 3 or n in SCALAR_TAKES_ALL:
                    nc.scalar.copy(out=dst, in_=src)
                else:
                    nc.vector.tensor_copy(out=dst, in_=src)

        def quantise_block(n, s):
            nc.vector.quantize_mx(
                out=cd[n][:, D * s : D * (s + 1)].bitcast(FP8X4),
                scales=pl[n][:, D * s : D * (s + 1)],
                in_=grouped[n][:, 4 * D * s : 4 * D * (s + 1)],
            )

        def mx_pass(bank, i_src, sign, n, s, start, stop):
            nc.tensor.matmul_mx(
                out=bank[:],
                lhsT=fcd[i_src][:, PAD + B * sign : PAD + B * (sign + 1)].bitcast(FP8X4),
                lhsT_scale=fpl[i_src][:, SLOT * sign : SLOT * sign + B],
                rhs=cd[n][:, D * s : D * (s + 1)].bitcast(FP8X4),
                rhs_scale=pl[n][:, D * s : D * (s + 1)],
                start=start,
                stop=stop,
            )

        def agg_passes(todo):
            for (dst, i_src) in todo:
                if agg_done[dst] == 0:
                    tag = "T0" if dst == NP - 1 else "A%d" % (dst % 2)
                    agg[dst] = psum.tile([P, D], F32, name="agg%d" % dst, tag=tag)
                if i_src < dst:
                    where, s = unit_of[(i_src, dst)], 0
                else:
                    where, s = unit_of[(dst, i_src)], 1
                mx_pass(agg[dst], i_src, 0, where, s, agg_done[dst] == 0, agg_done[dst] == NP - 2)
                agg_done[dst] += 1

        def multiply_unit(n):
            i, j = units[n]
            closes = [k for k in range(NP) if closed_in[k] == n]
            if closes:
                agg_passes(live[n])
                if n == n_units - 1:
                    agg_passes(early[n])
            dif[n] = psum.tile([P, D], F32, name="dif", tag="D")
            mx_pass(dif[n], i, 0, n, 0, True, False)
            mx_pass(dif[n], j, 1, n, 1, False, True)
            if not closes:
                agg_passes(live[n])
            if n < n_units - 1:
                agg_passes(early[n])
            return closes

        def square_unit(n):
            nc.scalar.activation(out=junk[:], in_=dif[n][:], func=ACT.Square, accum_out=acc[:, n : n + 1])

        def evacuate(j, on_scalar):
            aggT[j] = opool.tile([P, D], F32, name="aggT", tag="aggT")
            src = agg[j][:].rearrange("p (r e u a) -> p u e a r", r=2, e=2, u=2)
            for u in range(2):
                dst = aggT[j][:, 256 * u : 256 * (u + 1)].rearrange("p (e a r) -> p e a r", e=2, r=2)
                if on_scalar:
                    nc.scalar.mul(out=dst, in_=src[:, u], mul=0.125)
                else:
                    nc.vector.tensor_scalar_mul(out=dst, in0=src[:, u], scalar1=0.125)

        def transpose_back(j):
            tag = "X" if j < NP - 2 else "T%d" % (j - NP + 3)
            fin[j] = psum.tile([P, D], F32, name="fin%d" % j, tag=tag)
            for t in range(4):
                nc.tensor.transpose(fin[j][:, P * t : P * (t + 1)], aggT[j][:, P * t : P * (t + 1)], ident[:])

        def finish(j):
            res = opool.tile([P, D], F32, name="res", tag="res")
            nc.vector.scalar_tensor_tensor(
                out=res[:], in0=fm[:, j, :], scalar=0.125, in1=fin[j][:], op0=ALU.mult, op1=ALU.add
            )
            nc.sync.dma_start(
                out=out_0[j].rearrange("(u q e) b -> q u (e b)", u=2, e=2),
                in_=res[:].rearrange("p (u x) -> p u x", u=2),
            )

        load_unit(0)
        load_f(0)
        load_f(1)
        load_f(2)
        for n in range(1, RAW_BUFS):
            load_unit(n)
            if n + 2 < NP:
                load_f(n + 2)

        waiting = []
        for n in range(n_units - 1):
            transpose_unit(n)
            back = waiting
            for j in back:
                transpose_back(j)
            waiting = []
            if n >= 2:
                waiting = multiply_unit(n - 2)
                square_unit(n - 2)
                for j in waiting:
                    evacuate(j, False)
            new_f = [i for i in range(NP) if (i == 0 and n == 0) or i == n + 1]
            for i in new_f:
                regroup_f(i)
            quantise_block(n, 0)
            for i in new_f:
                negate_f(i)
            for i in new_f:
                quantise_f(i, 0)
            quantise_block(n, 1)
            for i in new_f:
                quantise_f(i, 1)
            for j in back:
                finish(j)
            if n + RAW_BUFS < n_units:
                load_unit(n + RAW_BUFS)
                if n + RAW_BUFS + 2 < NP:
                    load_f(n + RAW_BUFS + 2)

        n = n_units - 1
        transpose_unit(n)
        for j in waiting:
            transpose_back(j)
        quantise_block(n, 0)
        quantise_block(n, 1)
        for j in waiting:
            finish(j)
        multiply_unit(n - 2)
        square_unit(n - 2)
        multiply_unit(n - 1)
        square_unit(n - 1)
        evacuate(NP - 3, False)
        transpose_back(NP - 3)
        finish(NP - 3)
        multiply_unit(n)
        evacuate(NP - 2, False)
        evacuate(NP - 1, True)
        square_unit(n)
        transpose_back(NP - 2)
        transpose_back(NP - 1)
        finish(NP - 2)
        nc.vector.reduce_sum(out=zt[:, 0:1], in_=acc[:], axis=mybir.AxisListType.X)
        finish(NP - 1)

        lt = psum.tile([P, D], F32, name="lt", tag="T3")
        nc.tensor.transpose(lt[:, 0:P], zt[:], ident[:])
        nc.scalar.activation(out=junk[:, 0:P], in_=lt[:, 0:P], func=ACT.Copy, scale=LOSS_WEIGHT, accum_out=tot[:, 0:1])
        loss_view = out_1
        for k in range(2 - len(out_1.shape)):
            loss_view = loss_view.unsqueeze(0)
        nc.sync.dma_start(out=loss_view, in_=tot[0:1, 0:1])
